import numpy as np
import ml_dtypes


def mxq(x, axis, fmt="e4m3"):
    dtype, down = {"e4m3": (ml_dtypes.float8_e4m3fn, 7), "e5m2": (ml_dtypes.float8_e5m2, 14)}[fmt]
    v = np.moveaxis(np.asarray(x, np.float32).astype(ml_dtypes.bfloat16).astype(np.float64), axis, -1)
    blocks = v.reshape(v.shape[:-1] + (-1, 32))
    amax = np.abs(blocks).max(-1, keepdims=True)
    byte = np.maximum(np.where(amax > 0, np.frexp(amax)[1] - 1 + 127, 0) - down, 1)
    scale = np.exp2(byte - 127.0)
    codes = (blocks / scale).astype(np.float32).astype(dtype).astype(np.float64)
    return np.moveaxis((codes * scale).reshape(v.shape), -1, axis)


WIDE = False


def mx_kscale(k):
    if not WIDE:
        return np.ones(k)
    levels = np.array([10, -10, 5, -5, 0])
    a = np.random.permutation(np.resize(levels, k // 512 * 4)).reshape(k // 512, 4)
    idx = np.arange(k)
    return np.exp2(a[idx // 512, idx % 128 // 32])


BF16 = ml_dtypes.bfloat16


def bf(x):
    return np.asarray(x, np.float32).astype(BF16)


def f64(x):
    return np.asarray(x).astype(np.float64)


B, T, G, I, H = 2, 64, 8, 512, 256


def setup_inputs():
    s = mx_kscale(I)
    return {"x": bf((np.random.standard_normal((B, T, G, I)) * s).reshape(B, T, G * I)),
            "W": bf(np.random.standard_normal((G, H, I)) / np.sqrt(I) / s),
            "b": bf(np.random.standard_normal((G, H)) * 0.5)}


def reference(x, W, b):
    xg = f64(x).reshape(B, T, G, I)
    xq = mxq(xg, 3, "e4m3")
    wq = mxq(f64(W), 2, "e4m3")
    y = xq.transpose(2, 0, 1, 3).reshape(G, B * T, I) @ wq.transpose(0, 2, 1)
    out = y.reshape(G, B, T, H).transpose(1, 2, 0, 3) + f64(b)
    return np.swapaxes(out, -1, -2).reshape(B, T, G * H)

@@ -1,0 +1,112 @@
+import concourse.mybir as mybir
+from concourse.masks import make_identity
+
+F32 = mybir.dt.float32
+BF16 = mybir.dt.bfloat16
+U32 = mybir.dt.uint32
+U8 = mybir.dt.uint8
+FP8X4 = mybir.dt.float8_e4m3fn_x4
+
+P = 128
+G = 8
+I = 512
+H = 256
+QUAD = 4
+WORDS = I // 2
+H_HALVES = H // P
+
+FLOPS = 2 * P * G * I * H
+
+
+def tile_groupedlinear_s_kernel(tc, x, W, b, out):
+    nc = tc.nc
+    x_rows = x.flatten_outer_dims()
+    out_rows = out.flatten_outer_dims()
+
+    with tc.tile_pool(name="const", bufs=1) as const, tc.tile_pool(
+        name="raw", bufs=6
+    ) as raw_pool, tc.tile_pool(name="stage", bufs=4) as stage, tc.tile_pool(
+        name="keep", bufs=6
+    ) as keep, tc.tile_pool(name="result", bufs=2) as result, tc.psum_pool(
+        name="flipped", bufs=4
+    ) as flipped, tc.psum_pool(name="sums", bufs=4) as sums:
+
+        ident = const.tile([P, P], F32)
+        make_identity(nc, ident[:])
+
+        bias = const.tile([P, G * H], BF16)
+        nc.scalar.dma_start(out=bias[:], in_=b.rearrange("g h -> (g h)").partition_broadcast(P))
+        bias_gh = bias[:].rearrange("p (g h) -> p g h", g=G)
+
+        def load_chunk(rows):
+            raw = raw_pool.tile([P, QUAD * I], BF16)
+            nc.sync.dma_start(out=raw[:].rearrange("p (g k) -> p g k", g=QUAD), in_=rows)
+            return raw
+
+        def transpose_and_quantise(raw):
+            codes = keep.tile([P, QUAD * P], U32, align_bytes=64)
+            scales = keep.tile([P, QUAD * P], U8, align_bytes=64)
+            words = raw[:].bitcast(F32)
+            for pair in range(QUAD // 2):
+                bank = flipped.tile([P, 2, 2, P], F32)
+                for g in range(2):
+                    for u in range(2):
+                        first = ((2 * pair + g) * 2 + u) * P
+                        nc.tensor.transpose(bank[:, g, u, :], words[:, first : first + P], ident[:])
+                grouped = stage.tile([P, 2 * P * 4], BF16, align_bytes=64)
+                nc.scalar.copy(
+                    out=grouped[:].bitcast(F32).rearrange("p (g r u) -> p g r u", g=2, u=2),
+                    in_=bank[:].rearrange("p g u r -> p g r u"),
+                )
+                cols = slice(pair * 2 * P, (pair + 1) * 2 * P)
+                nc.vector.quantize_mx(
+                    out=codes[:, cols].bitcast(FP8X4), scales=scales[:, cols], in_=grouped[:]
+                )
+            return codes, scales
+
+        def x_chunk(q):
+            return x_rows[:, q * QUAD * I : (q + 1) * QUAD * I].rearrange("n (g k) -> n g k", g=QUAD)
+
+        def w_chunk(j, q):
+            return W[q * QUAD : (q + 1) * QUAD, j * P : (j + 1) * P, :].rearrange("g h k -> h g k")
+
+        x_raw = {}
+        w_raw = {}
+        x_raw[0] = load_chunk(x_chunk(0))
+        w_raw[(0, 0)] = load_chunk(w_chunk(0, 0))
+        x_raw[1] = load_chunk(x_chunk(1))
+        w_raw[(0, 1)] = load_chunk(w_chunk(0, 1))
+        w_raw[(1, 0)] = load_chunk(w_chunk(1, 0))
+        w_raw[(1, 1)] = load_chunk(w_chunk(1, 1))
+
+        x_mx = {}
+        for j in range(H_HALVES):
+            shuffled = result.tile([P, P, G], F32)
+            for q in range(G // QUAD):
+                if j == 0:
+                    x_mx[q] = transpose_and_quantise(x_raw[q])
+                x_codes, x_scales = x_mx[q]
+                w_codes, w_scales = transpose_and_quantise(w_raw[(j, q)])
+                acc = sums.tile([P, QUAD, P], F32)
+                for g in range(QUAD):
+                    cols = slice(g * P, (g + 1) * P)
+                    nc.tensor.matmul_mx(
+                        out=acc[:, g, :],
+                        lhsT=x_codes[:, cols].bitcast(FP8X4),
+                        lhsT_scale=x_scales[:, cols],
+                        rhs=w_codes[:, cols].bitcast(FP8X4),
+                        rhs_scale=w_scales[:, cols],
+                        start=True,
+                        stop=True,
+                    )
+                groups = slice(q * QUAD, (q + 1) * QUAD)
+                nc.vector.tensor_tensor(
+                    out=shuffled[:, :, groups],
+                    in0=acc[:].rearrange("p g h -> p h g"),
+                    in1=bias_gh[:, groups, j * P : (j + 1) * P].rearrange("p g h -> p h g"),
+                    op=mybir.AluOpType.add,
+                )
+            nc.sync.dma_start(
+                out=out_rows[:, j * P * G : (j + 1) * P * G],
+                in_=shuffled[:].rearrange("p h g -> p (h g)"),
+            )

@@ -14,6 +14,7 @@ H = 256
 QUAD = 4
 WORDS = I // 2
 H_HALVES = H // P
+B_ROWS = G * H // P
 
 FLOPS = 2 * P * G * I * H
 
@@ -34,8 +35,28 @@ def tile_groupedlinear_s_kernel(tc, x, W, b, out):
         ident = const.tile([P, P], F32)
         make_identity(nc, ident[:])
 
+        ident_bf = const.tile([P, P], BF16)
+        make_identity(nc, ident_bf[:])
+
+        b_rows = const.tile([P, P], BF16)
+        nc.vector.memset(b_rows[:], 0.0)
+        nc.scalar.dma_start(out=b_rows[0:B_ROWS, :], in_=b.rearrange("g (j h) -> (g j) h", h=P))
+        b_flipped = flipped.tile([P, P], BF16, tag="bank")
+        nc.tensor.transpose(b_flipped[:], b_rows[:], ident_bf[:])
+        b_cols = const.tile([P, B_ROWS], BF16)
+        nc.vector.tensor_copy(out=b_cols[:], in_=b_flipped[:, 0:B_ROWS])
         bias = const.tile([P, G * H], BF16)
-        nc.scalar.dma_start(out=bias[:], in_=b.rearrange("g h -> (g h)").partition_broadcast(P))
+        for half in range(2):
+            spread = flipped.tile([P, B_ROWS // 2, P], BF16, tag="bank")
+            for k in range(B_ROWS // 2):
+                c = half * (B_ROWS // 2) + k
+                nc.tensor.transpose(
+                    spread[:, k, :], b_cols[:, c : c + 1].to_broadcast([P, P]), ident_bf[:]
+                )
+            nc.vector.tensor_copy(
+                out=bias[:, half * G * P : (half + 1) * G * P],
+                in_=spread[:].rearrange("p k n -> p (k n)"),
+            )
         bias_gh = bias[:].rearrange("p (g h) -> p g h", g=G)
 
         def load_chunk(rows):
@@ -48,7 +69,7 @@ def tile_groupedlinear_s_kernel(tc, x, W, b, out):
             scales = keep.tile([P, QUAD * P], U8, align_bytes=64)
             words = raw[:].bitcast(F32)
             for pair in range(QUAD // 2):
-                bank = flipped.tile([P, 2, 2, P], F32)
+                bank = flipped.tile([P, 2, 2, P], F32, tag="bank")
                 for g in range(2):
                     for u in range(2):
                         first = ((2 * pair + g) * 2 + u) * P

@@ -12,9 +12,10 @@ G = 8
 I = 512
 H = 256
 QUAD = 4
-WORDS = I // 2
 H_HALVES = H // P
-B_ROWS = G * H // P
+WIDE = 512
+WARM_PASSES = 8
+BUNCH_COLUMNS = 1024
 
 FLOPS = 2 * P * G * I * H
 
@@ -30,46 +31,60 @@ def tile_groupedlinear_s_kernel(tc, x, W, b, out):
         name="keep", bufs=6
     ) as keep, tc.tile_pool(name="result", bufs=2) as result, tc.psum_pool(
         name="flipped", bufs=4
-    ) as flipped, tc.psum_pool(name="sums", bufs=4) as sums:
-
-        ident = const.tile([P, P], F32)
-        make_identity(nc, ident[:])
-
-        ident_bf = const.tile([P, P], BF16)
-        make_identity(nc, ident_bf[:])
-
-        b_rows = const.tile([P, P], BF16)
-        nc.vector.memset(b_rows[:], 0.0)
-        nc.scalar.dma_start(out=b_rows[0:B_ROWS, :], in_=b.rearrange("g (j h) -> (g j) h", h=P))
-        b_flipped = flipped.tile([P, P], BF16, tag="bank")
-        nc.tensor.transpose(b_flipped[:], b_rows[:], ident_bf[:])
-        b_cols = const.tile([P, B_ROWS], BF16)
-        nc.vector.tensor_copy(out=b_cols[:], in_=b_flipped[:, 0:B_ROWS])
-        bias = const.tile([P, G * H], BF16)
-        for half in range(2):
-            spread = flipped.tile([P, B_ROWS // 2, P], BF16, tag="bank")
-            for k in range(B_ROWS // 2):
-                c = half * (B_ROWS // 2) + k
-                nc.tensor.transpose(
-                    spread[:, k, :], b_cols[:, c : c + 1].to_broadcast([P, P]), ident_bf[:]
-                )
-            nc.vector.tensor_copy(
-                out=bias[:, half * G * P : (half + 1) * G * P],
-                in_=spread[:].rearrange("p k n -> p (k n)"),
-            )
-        bias_gh = bias[:].rearrange("p (g h) -> p g h", g=G)
+    ) as flipped, tc.psum_pool(name="sums", bufs=3) as sums, tc.psum_pool(
+        name="unread", bufs=1
+    ) as unread, tc.manual_schedule():
 
         def load_chunk(rows):
             raw = raw_pool.tile([P, QUAD * I], BF16)
             nc.sync.dma_start(out=raw[:].rearrange("p (g k) -> p g k", g=QUAD), in_=rows)
             return raw
 
+        def x_chunk(q):
+            return x_rows[:, q * QUAD * I : (q + 1) * QUAD * I].rearrange("n (g k) -> n g k", g=QUAD)
+
+        def w_chunk(j, q):
+            return W[q * QUAD : (q + 1) * QUAD, j * P : (j + 1) * P, :].rearrange("g h k -> h g k")
+
+        x0_raw = load_chunk(x_chunk(0))
+        w00_raw = load_chunk(w_chunk(0, 0))
+        x1_raw = load_chunk(x_chunk(1))
+        w01_raw = load_chunk(w_chunk(0, 1))
+        w10_raw = load_chunk(w_chunk(1, 0))
+        w11_raw = load_chunk(w_chunk(1, 1))
+
+        bias = const.tile([P, G * H], BF16)
+        nc.scalar.dma_start(out=bias[:], in_=b.rearrange("g h -> (g h)").partition_broadcast(P))
+        bias_gh = bias[:].rearrange("p (g h) -> p g h", g=G)
+
+        ident = const.tile([P, P], F32)
+        make_identity(nc, ident[:])
+
+        zeros = const.tile([P, 4 * WIDE], BF16, align_bytes=64)
+        zero_codes = const.tile([P, WIDE], U32, align_bytes=64)
+        zero_scales = const.tile([P, WIDE], U8, align_bytes=64)
+        nc.vector.memset(zeros[:], 0.0)
+        nc.vector.quantize_mx(out=zero_codes[:].bitcast(FP8X4), scales=zero_scales[:], in_=zeros[:])
+        nothing = unread.tile([P, WIDE], F32)
+
+        def passes_on_zeros(count):
+            for n in range(count):
+                nc.tensor.matmul_mx(
+                    out=nothing[:],
+                    lhsT=zero_codes[:, 0:P].bitcast(FP8X4),
+                    lhsT_scale=zero_scales[:, 0:P],
+                    rhs=zero_codes[:].bitcast(FP8X4),
+                    rhs_scale=zero_scales[:],
+                    start=True,
+                    stop=True,
+                )
+
         def transpose_and_quantise(raw):
             codes = keep.tile([P, QUAD * P], U32, align_bytes=64)
             scales = keep.tile([P, QUAD * P], U8, align_bytes=64)
             words = raw[:].bitcast(F32)
             for pair in range(QUAD // 2):
-                bank = flipped.tile([P, 2, 2, P], F32, tag="bank")
+                bank = flipped.tile([P, 2, 2, P], F32)
                 for g in range(2):
                     for u in range(2):
                         first = ((2 * pair + g) * 2 + u) * P
@@ -85,49 +100,51 @@ def tile_groupedlinear_s_kernel(tc, x, W, b, out):
                 )
             return codes, scales
 
-        def x_chunk(q):
-            return x_rows[:, q * QUAD * I : (q + 1) * QUAD * I].rearrange("n (g k) -> n g k", g=QUAD)
-
-        def w_chunk(j, q):
-            return W[q * QUAD : (q + 1) * QUAD, j * P : (j + 1) * P, :].rearrange("g h k -> h g k")
-
-        x_raw = {}
-        w_raw = {}
-        x_raw[0] = load_chunk(x_chunk(0))
-        w_raw[(0, 0)] = load_chunk(w_chunk(0, 0))
-        x_raw[1] = load_chunk(x_chunk(1))
-        w_raw[(0, 1)] = load_chunk(w_chunk(0, 1))
-        w_raw[(1, 0)] = load_chunk(w_chunk(1, 0))
-        w_raw[(1, 1)] = load_chunk(w_chunk(1, 1))
-
-        x_mx = {}
-        for j in range(H_HALVES):
-            shuffled = result.tile([P, P, G], F32)
-            for q in range(G // QUAD):
-                if j == 0:
-                    x_mx[q] = transpose_and_quantise(x_raw[q])
-                x_codes, x_scales = x_mx[q]
-                w_codes, w_scales = transpose_and_quantise(w_raw[(j, q)])
-                acc = sums.tile([P, QUAD, P], F32)
-                for g in range(QUAD):
-                    cols = slice(g * P, (g + 1) * P)
-                    nc.tensor.matmul_mx(
-                        out=acc[:, g, :],
-                        lhsT=x_codes[:, cols].bitcast(FP8X4),
-                        lhsT_scale=x_scales[:, cols],
-                        rhs=w_codes[:, cols].bitcast(FP8X4),
-                        rhs_scale=w_scales[:, cols],
-                        start=True,
-                        stop=True,
-                    )
-                groups = slice(q * QUAD, (q + 1) * QUAD)
-                nc.vector.tensor_tensor(
-                    out=shuffled[:, :, groups],
-                    in0=acc[:].rearrange("p g h -> p h g"),
-                    in1=bias_gh[:, groups, j * P : (j + 1) * P].rearrange("p g h -> p h g"),
-                    op=mybir.AluOpType.add,
+        def multiply(x_mx, w_mx, shuffled, j, q):
+            x_codes, x_scales = x_mx
+            w_codes, w_scales = w_mx
+            acc = sums.tile([P, QUAD, P], F32)
+            for g in range(QUAD):
+                cols = slice(g * P, (g + 1) * P)
+                nc.tensor.matmul_mx(
+                    out=acc[:, g, :],
+                    lhsT=x_codes[:, cols].bitcast(FP8X4),
+                    lhsT_scale=x_scales[:, cols],
+                    rhs=w_codes[:, cols].bitcast(FP8X4),
+                    rhs_scale=w_scales[:, cols],
+                    start=True,
+                    stop=True,
                 )
+            passes_on_zeros((BUNCH_COLUMNS - QUAD * P) // WIDE)
+            groups = slice(q * QUAD, (q + 1) * QUAD)
+            nc.vector.tensor_tensor(
+                out=shuffled[:, :, groups],
+                in0=acc[:].rearrange("p g h -> p h g"),
+                in1=bias_gh[:, groups, j * P : (j + 1) * P].rearrange("p g h -> p h g"),
+                op=mybir.AluOpType.add,
+            )
+
+        def store(shuffled, j):
             nc.sync.dma_start(
                 out=out_rows[:, j * P * G : (j + 1) * P * G],
                 in_=shuffled[:].rearrange("p h g -> p (h g)"),
             )
+
+        first_half = result.tile([P, P, G], F32)
+        second_half = result.tile([P, P, G], F32)
+        passes_on_zeros(WARM_PASSES)
+        x0 = transpose_and_quantise(x0_raw)
+        passes_on_zeros(BUNCH_COLUMNS // WIDE)
+        w00 = transpose_and_quantise(w00_raw)
+        passes_on_zeros(BUNCH_COLUMNS // WIDE)
+        x1 = transpose_and_quantise(x1_raw)
+        multiply(x0, w00, first_half, 0, 0)
+        w01 = transpose_and_quantise(w01_raw)
+        passes_on_zeros(BUNCH_COLUMNS // WIDE)
+        w10 = transpose_and_quantise(w10_raw)
+        multiply(x1, w01, first_half, 0, 1)
+        store(first_half, 0)
+        w11 = transpose_and_quantise(w11_raw)
+        multiply(x0, w10, second_half, 1, 0)
+        multiply(x1, w11, second_half, 1, 1)
+        store(second_half, 1)

@@ -13,9 +13,6 @@ I = 512
 H = 256
 QUAD = 4
 H_HALVES = H // P
-WIDE = 512
-WARM_PASSES = 8
-BUNCH_COLUMNS = 1024
 
 FLOPS = 2 * P * G * I * H
 
@@ -31,9 +28,7 @@ def tile_groupedlinear_s_kernel(tc, x, W, b, out):
         name="keep", bufs=6
     ) as keep, tc.tile_pool(name="result", bufs=2) as result, tc.psum_pool(
         name="flipped", bufs=4
-    ) as flipped, tc.psum_pool(name="sums", bufs=3) as sums, tc.psum_pool(
-        name="unread", bufs=1
-    ) as unread, tc.manual_schedule():
+    ) as flipped, tc.psum_pool(name="sums", bufs=4) as sums, tc.manual_schedule():
 
         def load_chunk(rows):
             raw = raw_pool.tile([P, QUAD * I], BF16)
@@ -59,25 +54,6 @@ def tile_groupedlinear_s_kernel(tc, x, W, b, out):
 
         ident = const.tile([P, P], F32)
         make_identity(nc, ident[:])
-
-        zeros = const.tile([P, 4 * WIDE], BF16, align_bytes=64)
-        zero_codes = const.tile([P, WIDE], U32, align_bytes=64)
-        zero_scales = const.tile([P, WIDE], U8, align_bytes=64)
-        nc.vector.memset(zeros[:], 0.0)
-        nc.vector.quantize_mx(out=zero_codes[:].bitcast(FP8X4), scales=zero_scales[:], in_=zeros[:])
-        nothing = unread.tile([P, WIDE], F32)
-
-        def passes_on_zeros(count):
-            for n in range(count):
-                nc.tensor.matmul_mx(
-                    out=nothing[:],
-                    lhsT=zero_codes[:, 0:P].bitcast(FP8X4),
-                    lhsT_scale=zero_scales[:, 0:P],
-                    rhs=zero_codes[:].bitcast(FP8X4),
-                    rhs_scale=zero_scales[:],
-                    start=True,
-                    stop=True,
-                )
 
         def transpose_and_quantise(raw):
             codes = keep.tile([P, QUAD * P], U32, align_bytes=64)
@@ -115,7 +91,6 @@ def tile_groupedlinear_s_kernel(tc, x, W, b, out):
                     start=True,
                     stop=True,
                 )
-            passes_on_zeros((BUNCH_COLUMNS - QUAD * P) // WIDE)
             groups = slice(q * QUAD, (q + 1) * QUAD)
             nc.vector.tensor_tensor(
                 out=shuffled[:, :, groups],
@@ -132,15 +107,11 @@ def tile_groupedlinear_s_kernel(tc, x, W, b, out):
 
         first_half = result.tile([P, P, G], F32)
         second_half = result.tile([P, P, G], F32)
-        passes_on_zeros(WARM_PASSES)
         x0 = transpose_and_quantise(x0_raw)
-        passes_on_zeros(BUNCH_COLUMNS // WIDE)
         w00 = transpose_and_quantise(w00_raw)
-        passes_on_zeros(BUNCH_COLUMNS // WIDE)
         x1 = transpose_and_quantise(x1_raw)
         multiply(x0, w00, first_half, 0, 0)
         w01 = transpose_and_quantise(w01_raw)
-        passes_on_zeros(BUNCH_COLUMNS // WIDE)
         w10 = transpose_and_quantise(w10_raw)
         multiply(x1, w01, first_half, 0, 1)
         store(first_half, 0)

@@ -3,6 +3,7 @@ from concourse.masks import make_identity
 
 F32 = mybir.dt.float32
 BF16 = mybir.dt.bfloat16
+I32 = mybir.dt.int32
 U32 = mybir.dt.uint32
 U8 = mybir.dt.uint8
 FP8X4 = mybir.dt.float8_e4m3fn_x4
@@ -13,6 +14,10 @@ I = 512
 H = 256
 QUAD = 4
 H_HALVES = H // P
+B_ROWS = G * H // P
+WIDE = 512
+WARM_PASSES = 4
+BUNCH_COLUMNS = 1024
 
 FLOPS = 2 * P * G * I * H
 
@@ -28,7 +33,9 @@ def tile_groupedlinear_s_kernel(tc, x, W, b, out):
         name="keep", bufs=6
     ) as keep, tc.tile_pool(name="result", bufs=2) as result, tc.psum_pool(
         name="flipped", bufs=4
-    ) as flipped, tc.psum_pool(name="sums", bufs=4) as sums, tc.manual_schedule():
+    ) as flipped, tc.psum_pool(name="sums", bufs=3) as sums, tc.psum_pool(
+        name="unread", bufs=1
+    ) as unread, tc.manual_schedule():
 
         def load_chunk(rows):
             raw = raw_pool.tile([P, QUAD * I], BF16)
@@ -41,6 +48,9 @@ def tile_groupedlinear_s_kernel(tc, x, W, b, out):
         def w_chunk(j, q):
             return W[q * QUAD : (q + 1) * QUAD, j * P : (j + 1) * P, :].rearrange("g h k -> h g k")
 
+        b_rows = const.tile([P, P], BF16)
+        nc.vector.memset(b_rows[:], 0.0)
+        nc.sync.dma_start(out=b_rows[0:B_ROWS, :], in_=b.rearrange("g (j h) -> (g j) h", h=P))
         x0_raw = load_chunk(x_chunk(0))
         w00_raw = load_chunk(w_chunk(0, 0))
         x1_raw = load_chunk(x_chunk(1))
@@ -48,19 +58,36 @@ def tile_groupedlinear_s_kernel(tc, x, W, b, out):
         w10_raw = load_chunk(w_chunk(1, 0))
         w11_raw = load_chunk(w_chunk(1, 1))
 
-        bias = const.tile([P, G * H], BF16)
-        nc.scalar.dma_start(out=bias[:], in_=b.rearrange("g h -> (g h)").partition_broadcast(P))
-        bias_gh = bias[:].rearrange("p (g h) -> p g h", g=G)
-
+        ident_bf = const.tile([P, P], BF16)
+        make_identity(nc, ident_bf[:])
         ident = const.tile([P, P], F32)
         make_identity(nc, ident[:])
+
+        zeros = const.tile([P, 4 * WIDE], BF16, align_bytes=64)
+        zero_codes = const.tile([P, WIDE], U32, align_bytes=64)
+        zero_scales = const.tile([P, WIDE], U8, align_bytes=64)
+        nc.vector.memset(zeros[:].bitcast(I32), 0)
+        nc.vector.quantize_mx(out=zero_codes[:].bitcast(FP8X4), scales=zero_scales[:], in_=zeros[:])
+        nothing = unread.tile([P, WIDE], F32)
+
+        def passes_on_zeros(count):
+            for n in range(count):
+                nc.tensor.matmul_mx(
+                    out=nothing[:],
+                    lhsT=zero_codes[:, 0:P].bitcast(FP8X4),
+                    lhsT_scale=zero_scales[:, 0:P],
+                    rhs=zero_codes[:].bitcast(FP8X4),
+                    rhs_scale=zero_scales[:],
+                    start=True,
+                    stop=True,
+                )
 
         def transpose_and_quantise(raw):
             codes = keep.tile([P, QUAD * P], U32, align_bytes=64)
             scales = keep.tile([P, QUAD * P], U8, align_bytes=64)
             words = raw[:].bitcast(F32)
             for pair in range(QUAD // 2):
-                bank = flipped.tile([P, 2, 2, P], F32)
+                bank = flipped.tile([P, 2, 2, P], F32, tag="bank")
                 for g in range(2):
                     for u in range(2):
                         first = ((2 * pair + g) * 2 + u) * P
@@ -75,6 +102,25 @@ def tile_groupedlinear_s_kernel(tc, x, W, b, out):
                     out=codes[:, cols].bitcast(FP8X4), scales=scales[:, cols], in_=grouped[:]
                 )
             return codes, scales
+
+        def spread_bias():
+            b_flipped = flipped.tile([P, P], BF16, tag="bank")
+            nc.tensor.transpose(b_flipped[:], b_rows[:], ident_bf[:])
+            b_cols = const.tile([P, B_ROWS], BF16)
+            nc.vector.tensor_copy(out=b_cols[:], in_=b_flipped[:, 0:B_ROWS])
+            bias = const.tile([P, G * H], BF16)
+            for half in range(2):
+                spread = flipped.tile([P, B_ROWS // 2, P], BF16, tag="bank")
+                for k in range(B_ROWS // 2):
+                    c = half * (B_ROWS // 2) + k
+                    nc.tensor.transpose(
+                        spread[:, k, :], b_cols[:, c : c + 1].to_broadcast([P, P]), ident_bf[:]
+                    )
+                nc.vector.tensor_copy(
+                    out=bias[:, half * G * P : (half + 1) * G * P],
+                    in_=spread[:].rearrange("p k n -> p (k n)"),
+                )
+            return bias[:].rearrange("p (g h) -> p g h", g=G)
 
         def multiply(x_mx, w_mx, shuffled, j, q):
             x_codes, x_scales = x_mx
@@ -91,6 +137,7 @@ def tile_groupedlinear_s_kernel(tc, x, W, b, out):
                     start=True,
                     stop=True,
                 )
+            passes_on_zeros((BUNCH_COLUMNS - QUAD * P) // WIDE)
             groups = slice(q * QUAD, (q + 1) * QUAD)
             nc.vector.tensor_tensor(
                 out=shuffled[:, :, groups],
@@ -107,11 +154,16 @@ def tile_groupedlinear_s_kernel(tc, x, W, b, out):
 
         first_half = result.tile([P, P, G], F32)
         second_half = result.tile([P, P, G], F32)
+        passes_on_zeros(WARM_PASSES)
+        bias_gh = spread_bias()
         x0 = transpose_and_quantise(x0_raw)
+        passes_on_zeros(BUNCH_COLUMNS // WIDE)
         w00 = transpose_and_quantise(w00_raw)
+        passes_on_zeros(BUNCH_COLUMNS // WIDE)
         x1 = transpose_and_quantise(x1_raw)
         multiply(x0, w00, first_half, 0, 0)
         w01 = transpose_and_quantise(w01_raw)
+        passes_on_zeros(BUNCH_COLUMNS // WIDE)
         w10 = transpose_and_quantise(w10_raw)
         multiply(x1, w01, first_half, 0, 1)
         store(first_half, 0)

@@ -13,10 +13,8 @@ G = 8
 I = 512
 H = 256
 QUAD = 4
-H_HALVES = H // P
-B_ROWS = G * H // P
-WIDE = 512
-WARM_PASSES = 4
+WIDE = 256
+WARM_COLUMNS = 12 * WIDE
 BUNCH_COLUMNS = 1024
 
 FLOPS = 2 * P * G * I * H
@@ -31,7 +29,7 @@ def tile_groupedlinear_s_kernel(tc, x, W, b, out):
         name="raw", bufs=6
     ) as raw_pool, tc.tile_pool(name="stage", bufs=4) as stage, tc.tile_pool(
         name="keep", bufs=6
-    ) as keep, tc.tile_pool(name="result", bufs=2) as result, tc.psum_pool(
+    ) as keep, tc.tile_pool(name="result", bufs=1) as result, tc.psum_pool(
         name="flipped", bufs=4
     ) as flipped, tc.psum_pool(name="sums", bufs=3) as sums, tc.psum_pool(
         name="unread", bufs=1
@@ -48,18 +46,16 @@ def tile_groupedlinear_s_kernel(tc, x, W, b, out):
         def w_chunk(j, q):
             return W[q * QUAD : (q + 1) * QUAD, j * P : (j + 1) * P, :].rearrange("g h k -> h g k")
 
-        b_rows = const.tile([P, P], BF16)
-        nc.vector.memset(b_rows[:], 0.0)
-        nc.sync.dma_start(out=b_rows[0:B_ROWS, :], in_=b.rearrange("g (j h) -> (g j) h", h=P))
         x0_raw = load_chunk(x_chunk(0))
         w00_raw = load_chunk(w_chunk(0, 0))
         x1_raw = load_chunk(x_chunk(1))
+        bias = const.tile([P, G * H], BF16)
+        nc.sync.dma_start(out=bias[:], in_=b.rearrange("g h -> (g h)").partition_broadcast(P))
+        bias_gh = bias[:].rearrange("p (g h) -> p g h", g=G)
         w01_raw = load_chunk(w_chunk(0, 1))
         w10_raw = load_chunk(w_chunk(1, 0))
         w11_raw = load_chunk(w_chunk(1, 1))
 
-        ident_bf = const.tile([P, P], BF16)
-        make_identity(nc, ident_bf[:])
         ident = const.tile([P, P], F32)
         make_identity(nc, ident[:])
 
@@ -70,8 +66,8 @@ def tile_groupedlinear_s_kernel(tc, x, W, b, out):
         nc.vector.quantize_mx(out=zero_codes[:].bitcast(FP8X4), scales=zero_scales[:], in_=zeros[:])
         nothing = unread.tile([P, WIDE], F32)
 
-        def passes_on_zeros(count):
-            for n in range(count):
+        def passes_on_zeros(columns):
+            for n in range(columns // WIDE):
                 nc.tensor.matmul_mx(
                     out=nothing[:],
                     lhsT=zero_codes[:, 0:P].bitcast(FP8X4),
@@ -87,7 +83,7 @@ def tile_groupedlinear_s_kernel(tc, x, W, b, out):
             scales = keep.tile([P, QUAD * P], U8, align_bytes=64)
             words = raw[:].bitcast(F32)
             for pair in range(QUAD // 2):
-                bank = flipped.tile([P, 2, 2, P], F32, tag="bank")
+                bank = flipped.tile([P, 2, 2, P], F32)
                 for g in range(2):
                     for u in range(2):
                         first = ((2 * pair + g) * 2 + u) * P
@@ -102,25 +98,6 @@ def tile_groupedlinear_s_kernel(tc, x, W, b, out):
                     out=codes[:, cols].bitcast(FP8X4), scales=scales[:, cols], in_=grouped[:]
                 )
             return codes, scales
-
-        def spread_bias():
-            b_flipped = flipped.tile([P, P], BF16, tag="bank")
-            nc.tensor.transpose(b_flipped[:], b_rows[:], ident_bf[:])
-            b_cols = const.tile([P, B_ROWS], BF16)
-            nc.vector.tensor_copy(out=b_cols[:], in_=b_flipped[:, 0:B_ROWS])
-            bias = const.tile([P, G * H], BF16)
-            for half in range(2):
-                spread = flipped.tile([P, B_ROWS // 2, P], BF16, tag="bank")
-                for k in range(B_ROWS // 2):
-                    c = half * (B_ROWS // 2) + k
-                    nc.tensor.transpose(
-                        spread[:, k, :], b_cols[:, c : c + 1].to_broadcast([P, P]), ident_bf[:]
-                    )
-                nc.vector.tensor_copy(
-                    out=bias[:, half * G * P : (half + 1) * G * P],
-                    in_=spread[:].rearrange("p k n -> p (k n)"),
-                )
-            return bias[:].rearrange("p (g h) -> p g h", g=G)
 
         def multiply(x_mx, w_mx, shuffled, j, q):
             x_codes, x_scales = x_mx
@@ -137,7 +114,6 @@ def tile_groupedlinear_s_kernel(tc, x, W, b, out):
                     start=True,
                     stop=True,
                 )
-            passes_on_zeros((BUNCH_COLUMNS - QUAD * P) // WIDE)
             groups = slice(q * QUAD, (q + 1) * QUAD)
             nc.vector.tensor_tensor(
                 out=shuffled[:, :, groups],
@@ -154,18 +130,20 @@ def tile_groupedlinear_s_kernel(tc, x, W, b, out):
 
         first_half = result.tile([P, P, G], F32)
         second_half = result.tile([P, P, G], F32)
-        passes_on_zeros(WARM_PASSES)
-        bias_gh = spread_bias()
+        real_columns = QUAD * P
+        passes_on_zeros(WARM_COLUMNS)
         x0 = transpose_and_quantise(x0_raw)
-        passes_on_zeros(BUNCH_COLUMNS // WIDE)
+        passes_on_zeros(BUNCH_COLUMNS)
         w00 = transpose_and_quantise(w00_raw)
-        passes_on_zeros(BUNCH_COLUMNS // WIDE)
+        passes_on_zeros(BUNCH_COLUMNS)
         x1 = transpose_and_quantise(x1_raw)
         multiply(x0, w00, first_half, 0, 0)
+        passes_on_zeros(BUNCH_COLUMNS - real_columns)
         w01 = transpose_and_quantise(w01_raw)
-        passes_on_zeros(BUNCH_COLUMNS // WIDE)
+        passes_on_zeros(BUNCH_COLUMNS)
         w10 = transpose_and_quantise(w10_raw)
         multiply(x1, w01, first_half, 0, 1)
+        passes_on_zeros(BUNCH_COLUMNS - real_columns)
         store(first_half, 0)
         w11 = transpose_and_quantise(w11_raw)
         multiply(x0, w10, second_half, 1, 0)

@@ -13,8 +13,11 @@ G = 8
 I = 512
 H = 256
 QUAD = 4
+PAIR = 2
+B_ROWS = G * H // P
+STORE_H = 64
 WIDE = 256
-WARM_COLUMNS = 12 * WIDE
+WARM_COLUMNS = 8 * WIDE
 BUNCH_COLUMNS = 1024
 
 FLOPS = 2 * P * G * I * H
@@ -26,36 +29,41 @@ def tile_groupedlinear_s_kernel(tc, x, W, b, out):
     out_rows = out.flatten_outer_dims()
 
     with tc.tile_pool(name="const", bufs=1) as const, tc.tile_pool(
-        name="raw", bufs=6
+        name="raw", bufs=7
     ) as raw_pool, tc.tile_pool(name="stage", bufs=4) as stage, tc.tile_pool(
         name="keep", bufs=6
-    ) as keep, tc.tile_pool(name="result", bufs=1) as result, tc.psum_pool(
+    ) as keep, tc.tile_pool(name="result", bufs=4) as result, tc.psum_pool(
         name="flipped", bufs=4
     ) as flipped, tc.psum_pool(name="sums", bufs=3) as sums, tc.psum_pool(
         name="unread", bufs=1
     ) as unread, tc.manual_schedule():
 
-        def load_chunk(rows):
-            raw = raw_pool.tile([P, QUAD * I], BF16)
-            nc.sync.dma_start(out=raw[:].rearrange("p (g k) -> p g k", g=QUAD), in_=rows)
+        def load(rows, groups):
+            raw = raw_pool.tile([P, groups * I], BF16)
+            nc.sync.dma_start(out=raw[:].rearrange("p (g k) -> p g k", g=groups), in_=rows)
             return raw
 
-        def x_chunk(q):
-            return x_rows[:, q * QUAD * I : (q + 1) * QUAD * I].rearrange("n (g k) -> n g k", g=QUAD)
+        def load_x(first, groups):
+            cols = slice(first * I, (first + groups) * I)
+            return load(x_rows[:, cols].rearrange("n (g k) -> n g k", g=groups), groups)
 
-        def w_chunk(j, q):
-            return W[q * QUAD : (q + 1) * QUAD, j * P : (j + 1) * P, :].rearrange("g h k -> h g k")
+        def load_w(j, first, groups):
+            rows = W[first : first + groups, j * P : (j + 1) * P, :]
+            return load(rows.rearrange("g h k -> h g k"), groups)
 
-        x0_raw = load_chunk(x_chunk(0))
-        w00_raw = load_chunk(w_chunk(0, 0))
-        x1_raw = load_chunk(x_chunk(1))
-        bias = const.tile([P, G * H], BF16)
-        nc.sync.dma_start(out=bias[:], in_=b.rearrange("g h -> (g h)").partition_broadcast(P))
-        bias_gh = bias[:].rearrange("p (g h) -> p g h", g=G)
-        w01_raw = load_chunk(w_chunk(0, 1))
-        w10_raw = load_chunk(w_chunk(1, 0))
-        w11_raw = load_chunk(w_chunk(1, 1))
+        b_rows = const.tile([P, P], BF16)
+        nc.gpsimd.memset(b_rows[:], 0.0)
+        nc.sync.dma_start(out=b_rows[0:B_ROWS, :], in_=b.rearrange("g (j h) -> (g j) h", h=P))
+        x0_raw = load_x(0, QUAD)
+        w00_raw = load_w(0, 0, QUAD)
+        x1_raw = load_x(QUAD, QUAD)
+        w01_raw = load_w(0, QUAD, QUAD)
+        w10_raw = load_w(1, 0, QUAD)
+        w11a_raw = load_w(1, QUAD, PAIR)
+        w11b_raw = load_w(1, QUAD + PAIR, PAIR)
 
+        ident_bf = const.tile([P, P], BF16)
+        make_identity(nc, ident_bf[:])
         ident = const.tile([P, P], F32)
         make_identity(nc, ident[:])
 
@@ -78,28 +86,51 @@ def tile_groupedlinear_s_kernel(tc, x, W, b, out):
                     stop=True,
                 )
 
-        def transpose_and_quantise(raw):
+        def transpose_and_quantise(pieces):
             codes = keep.tile([P, QUAD * P], U32, align_bytes=64)
             scales = keep.tile([P, QUAD * P], U8, align_bytes=64)
-            words = raw[:].bitcast(F32)
-            for pair in range(QUAD // 2):
-                bank = flipped.tile([P, 2, 2, P], F32)
-                for g in range(2):
+            pairs = []
+            for raw in pieces:
+                words = raw[:].bitcast(F32)
+                for first in range(0, words.shape[1], PAIR * I // 2):
+                    pairs.append(words[:, first : first + PAIR * I // 2])
+            for n, words in enumerate(pairs):
+                bank = flipped.tile([P, PAIR, 2, P], F32, tag="bank")
+                for g in range(PAIR):
                     for u in range(2):
-                        first = ((2 * pair + g) * 2 + u) * P
+                        first = (g * 2 + u) * P
                         nc.tensor.transpose(bank[:, g, u, :], words[:, first : first + P], ident[:])
-                grouped = stage.tile([P, 2 * P * 4], BF16, align_bytes=64)
+                grouped = stage.tile([P, PAIR * P * 4], BF16, align_bytes=64)
                 nc.scalar.copy(
-                    out=grouped[:].bitcast(F32).rearrange("p (g r u) -> p g r u", g=2, u=2),
+                    out=grouped[:].bitcast(F32).rearrange("p (g r u) -> p g r u", g=PAIR, u=2),
                     in_=bank[:].rearrange("p g u r -> p g r u"),
                 )
-                cols = slice(pair * 2 * P, (pair + 1) * 2 * P)
+                cols = slice(n * PAIR * P, (n + 1) * PAIR * P)
                 nc.vector.quantize_mx(
                     out=codes[:, cols].bitcast(FP8X4), scales=scales[:, cols], in_=grouped[:]
                 )
             return codes, scales
 
-        def multiply(x_mx, w_mx, shuffled, j, q):
+        def spread_bias():
+            b_flipped = flipped.tile([P, P], BF16, tag="bank")
+            nc.tensor.transpose(b_flipped[:], b_rows[:], ident_bf[:])
+            b_cols = const.tile([P, B_ROWS], BF16)
+            nc.vector.tensor_copy(out=b_cols[:], in_=b_flipped[:, 0:B_ROWS])
+            bias = const.tile([P, G * H], BF16)
+            for half in range(2):
+                spread = flipped.tile([P, B_ROWS // 2, P], BF16, tag="bank")
+                for k in range(B_ROWS // 2):
+                    c = half * (B_ROWS // 2) + k
+                    nc.tensor.transpose(
+                        spread[:, k, :], b_cols[:, c : c + 1].to_broadcast([P, P]), ident_bf[:]
+                    )
+                nc.vector.tensor_copy(
+                    out=bias[:, half * G * P : (half + 1) * G * P],
+                    in_=spread[:].rearrange("p k n -> p (k n)"),
+                )
+            return bias[:].rearrange("p (g h) -> p g h", g=G)
+
+        def multiply(x_mx, w_mx, parts, j, q):
             x_codes, x_scales = x_mx
             w_codes, w_scales = w_mx
             acc = sums.tile([P, QUAD, P], F32)
@@ -115,37 +146,47 @@ def tile_groupedlinear_s_kernel(tc, x, W, b, out):
                     stop=True,
                 )
             groups = slice(q * QUAD, (q + 1) * QUAD)
-            nc.vector.tensor_tensor(
-                out=shuffled[:, :, groups],
-                in0=acc[:].rearrange("p g h -> p h g"),
-                in1=bias_gh[:, groups, j * P : (j + 1) * P].rearrange("p g h -> p h g"),
-                op=mybir.AluOpType.add,
-            )
+            for n, shuffled in enumerate(parts):
+                first = n * STORE_H
+                nc.vector.tensor_tensor(
+                    out=shuffled[:, :, groups],
+                    in0=acc[:, :, first : first + STORE_H].rearrange("p g h -> p h g"),
+                    in1=bias_gh[:, groups, j * P + first : j * P + first + STORE_H].rearrange(
+                        "p g h -> p h g"
+                    ),
+                    op=mybir.AluOpType.add,
+                )
+                if q == G // QUAD - 1:
+                    cols = slice((j * P + first) * G, (j * P + first + STORE_H) * G)
+                    nc.sync.dma_start(
+                        out=out_rows[:, cols], in_=shuffled[:].rearrange("p h g -> p (h g)")
+                    )
 
-        def store(shuffled, j):
-            nc.sync.dma_start(
-                out=out_rows[:, j * P * G : (j + 1) * P * G],
-                in_=shuffled[:].rearrange("p h g -> p (h g)"),
-            )
+        def result_parts():
+            parts = []
+            for n in range(P // STORE_H):
+                shuffled = result.tile([P, STORE_H, G], F32)
+                parts.append(shuffled)
+            return parts
 
-        first_half = result.tile([P, P, G], F32)
-        second_half = result.tile([P, P, G], F32)
+        first_half = result_parts()
+        second_half = result_parts()
         real_columns = QUAD * P
         passes_on_zeros(WARM_COLUMNS)
-        x0 = transpose_and_quantise(x0_raw)
+        bias_gh = spread_bias()
         passes_on_zeros(BUNCH_COLUMNS)
-        w00 = transpose_and_quantise(w00_raw)
+        x0 = transpose_and_quantise([x0_raw])
         passes_on_zeros(BUNCH_COLUMNS)
-        x1 = transpose_and_quantise(x1_raw)
+        w00 = transpose_and_quantise([w00_raw])
+        passes_on_zeros(BUNCH_COLUMNS)
+        x1 = transpose_and_quantise([x1_raw])
         multiply(x0, w00, first_half, 0, 0)
         passes_on_zeros(BUNCH_COLUMNS - real_columns)
-        w01 = transpose_and_quantise(w01_raw)
+        w01 = transpose_and_quantise([w01_raw])
         passes_on_zeros(BUNCH_COLUMNS)
-        w10 = transpose_and_quantise(w10_raw)
+        w10 = transpose_and_quantise([w10_raw])
         multiply(x1, w01, first_half, 0, 1)
         passes_on_zeros(BUNCH_COLUMNS - real_columns)
-        store(first_half, 0)
-        w11 = transpose_and_quantise(w11_raw)
+        w11 = transpose_and_quantise([w11a_raw, w11b_raw])
         multiply(x0, w10, second_half, 1, 0)
         multiply(x1, w11, second_half, 1, 1)
-        store(second_half, 1)

@@ -3,7 +3,6 @@ from concourse.masks import make_identity
 
 F32 = mybir.dt.float32
 BF16 = mybir.dt.bfloat16
-I32 = mybir.dt.int32
 U32 = mybir.dt.uint32
 U8 = mybir.dt.uint8
 FP8X4 = mybir.dt.float8_e4m3fn_x4
@@ -13,12 +12,7 @@ G = 8
 I = 512
 H = 256
 QUAD = 4
-PAIR = 2
 B_ROWS = G * H // P
-STORE_H = 64
-WIDE = 256
-WARM_COLUMNS = 8 * WIDE
-BUNCH_COLUMNS = 1024
 
 FLOPS = 2 * P * G * I * H
 
@@ -29,83 +23,55 @@ def tile_groupedlinear_s_kernel(tc, x, W, b, out):
     out_rows = out.flatten_outer_dims()
 
     with tc.tile_pool(name="const", bufs=1) as const, tc.tile_pool(
-        name="raw", bufs=7
+        name="raw", bufs=6
     ) as raw_pool, tc.tile_pool(name="stage", bufs=4) as stage, tc.tile_pool(
         name="keep", bufs=6
-    ) as keep, tc.tile_pool(name="result", bufs=4) as result, tc.psum_pool(
+    ) as keep, tc.tile_pool(name="result", bufs=1) as result, tc.psum_pool(
         name="flipped", bufs=4
-    ) as flipped, tc.psum_pool(name="sums", bufs=3) as sums, tc.psum_pool(
-        name="unread", bufs=1
-    ) as unread, tc.manual_schedule():
+    ) as flipped, tc.psum_pool(name="sums", bufs=4) as sums, tc.manual_schedule():
 
-        def load(rows, groups):
-            raw = raw_pool.tile([P, groups * I], BF16)
-            nc.sync.dma_start(out=raw[:].rearrange("p (g k) -> p g k", g=groups), in_=rows)
+        def load_chunk(rows):
+            raw = raw_pool.tile([P, QUAD * I], BF16)
+            nc.sync.dma_start(out=raw[:].rearrange("p (g k) -> p g k", g=QUAD), in_=rows)
             return raw
 
-        def load_x(first, groups):
-            cols = slice(first * I, (first + groups) * I)
-            return load(x_rows[:, cols].rearrange("n (g k) -> n g k", g=groups), groups)
+        def x_chunk(q):
+            return x_rows[:, q * QUAD * I : (q + 1) * QUAD * I].rearrange("n (g k) -> n g k", g=QUAD)
 
-        def load_w(j, first, groups):
-            rows = W[first : first + groups, j * P : (j + 1) * P, :]
-            return load(rows.rearrange("g h k -> h g k"), groups)
+        def w_chunk(j, q):
+            return W[q * QUAD : (q + 1) * QUAD, j * P : (j + 1) * P, :].rearrange("g h k -> h g k")
 
         b_rows = const.tile([P, P], BF16)
         nc.gpsimd.memset(b_rows[:], 0.0)
         nc.sync.dma_start(out=b_rows[0:B_ROWS, :], in_=b.rearrange("g (j h) -> (g j) h", h=P))
-        x0_raw = load_x(0, QUAD)
-        w00_raw = load_w(0, 0, QUAD)
-        x1_raw = load_x(QUAD, QUAD)
-        w01_raw = load_w(0, QUAD, QUAD)
-        w10_raw = load_w(1, 0, QUAD)
-        w11a_raw = load_w(1, QUAD, PAIR)
-        w11b_raw = load_w(1, QUAD + PAIR, PAIR)
+        x0_raw = load_chunk(x_chunk(0))
+        w00_raw = load_chunk(w_chunk(0, 0))
+        x1_raw = load_chunk(x_chunk(1))
+        w01_raw = load_chunk(w_chunk(0, 1))
+        w10_raw = load_chunk(w_chunk(1, 0))
+        w11_raw = load_chunk(w_chunk(1, 1))
 
         ident_bf = const.tile([P, P], BF16)
         make_identity(nc, ident_bf[:])
         ident = const.tile([P, P], F32)
         make_identity(nc, ident[:])
 
-        zeros = const.tile([P, 4 * WIDE], BF16, align_bytes=64)
-        zero_codes = const.tile([P, WIDE], U32, align_bytes=64)
-        zero_scales = const.tile([P, WIDE], U8, align_bytes=64)
-        nc.vector.memset(zeros[:].bitcast(I32), 0)
-        nc.vector.quantize_mx(out=zero_codes[:].bitcast(FP8X4), scales=zero_scales[:], in_=zeros[:])
-        nothing = unread.tile([P, WIDE], F32)
-
-        def passes_on_zeros(columns):
-            for n in range(columns // WIDE):
-                nc.tensor.matmul_mx(
-                    out=nothing[:],
-                    lhsT=zero_codes[:, 0:P].bitcast(FP8X4),
-                    lhsT_scale=zero_scales[:, 0:P],
-                    rhs=zero_codes[:].bitcast(FP8X4),
-                    rhs_scale=zero_scales[:],
-                    start=True,
-                    stop=True,
-                )
-
-        def transpose_and_quantise(pieces):
+        def transpose_and_quantise(raw):
             codes = keep.tile([P, QUAD * P], U32, align_bytes=64)
             scales = keep.tile([P, QUAD * P], U8, align_bytes=64)
-            pairs = []
-            for raw in pieces:
-                words = raw[:].bitcast(F32)
-                for first in range(0, words.shape[1], PAIR * I // 2):
-                    pairs.append(words[:, first : first + PAIR * I // 2])
-            for n, words in enumerate(pairs):
-                bank = flipped.tile([P, PAIR, 2, P], F32, tag="bank")
-                for g in range(PAIR):
+            words = raw[:].bitcast(F32)
+            for pair in range(QUAD // 2):
+                bank = flipped.tile([P, 2, 2, P], F32, tag="bank")
+                for g in range(2):
                     for u in range(2):
-                        first = (g * 2 + u) * P
+                        first = ((2 * pair + g) * 2 + u) * P
                         nc.tensor.transpose(bank[:, g, u, :], words[:, first : first + P], ident[:])
-                grouped = stage.tile([P, PAIR * P * 4], BF16, align_bytes=64)
+                grouped = stage.tile([P, 2 * P * 4], BF16, align_bytes=64)
                 nc.scalar.copy(
-                    out=grouped[:].bitcast(F32).rearrange("p (g r u) -> p g r u", g=PAIR, u=2),
+                    out=grouped[:].bitcast(F32).rearrange("p (g r u) -> p g r u", g=2, u=2),
                     in_=bank[:].rearrange("p g u r -> p g r u"),
                 )
-                cols = slice(n * PAIR * P, (n + 1) * PAIR * P)
+                cols = slice(pair * 2 * P, (pair + 1) * 2 * P)
                 nc.vector.quantize_mx(
                     out=codes[:, cols].bitcast(FP8X4), scales=scales[:, cols], in_=grouped[:]
                 )
@@ -130,7 +96,7 @@ def tile_groupedlinear_s_kernel(tc, x, W, b, out):
                 )
             return bias[:].rearrange("p (g h) -> p g h", g=G)
 
-        def multiply(x_mx, w_mx, parts, j, q):
+        def multiply(x_mx, w_mx, shuffled, j, q):
             x_codes, x_scales = x_mx
             w_codes, w_scales = w_mx
             acc = sums.tile([P, QUAD, P], F32)
@@ -146,47 +112,31 @@ def tile_groupedlinear_s_kernel(tc, x, W, b, out):
                     stop=True,
                 )
             groups = slice(q * QUAD, (q + 1) * QUAD)
-            for n, shuffled in enumerate(parts):
-                first = n * STORE_H
-                nc.vector.tensor_tensor(
-                    out=shuffled[:, :, groups],
-                    in0=acc[:, :, first : first + STORE_H].rearrange("p g h -> p h g"),
-                    in1=bias_gh[:, groups, j * P + first : j * P + first + STORE_H].rearrange(
-                        "p g h -> p h g"
-                    ),
-                    op=mybir.AluOpType.add,
-                )
-                if q == G // QUAD - 1:
-                    cols = slice((j * P + first) * G, (j * P + first + STORE_H) * G)
-                    nc.sync.dma_start(
-                        out=out_rows[:, cols], in_=shuffled[:].rearrange("p h g -> p (h g)")
-                    )
+            nc.vector.tensor_tensor(
+                out=shuffled[:, :, groups],
+                in0=acc[:].rearrange("p g h -> p h g"),
+                in1=bias_gh[:, groups, j * P : (j + 1) * P].rearrange("p g h -> p h g"),
+                op=mybir.AluOpType.add,
+            )
 
-        def result_parts():
-            parts = []
-            for n in range(P // STORE_H):
-                shuffled = result.tile([P, STORE_H, G], F32)
-                parts.append(shuffled)
-            return parts
+        def store(shuffled, j):
+            nc.sync.dma_start(
+                out=out_rows[:, j * P * G : (j + 1) * P * G],
+                in_=shuffled[:].rearrange("p h g -> p (h g)"),
+            )
 
-        first_half = result_parts()
-        second_half = result_parts()
-        real_columns = QUAD * P
-        passes_on_zeros(WARM_COLUMNS)
+        first_half = result.tile([P, P, G], F32)
+        second_half = result.tile([P, P, G], F32)
         bias_gh = spread_bias()
-        passes_on_zeros(BUNCH_COLUMNS)
-        x0 = transpose_and_quantise([x0_raw])
-        passes_on_zeros(BUNCH_COLUMNS)
-        w00 = transpose_and_quantise([w00_raw])
-        passes_on_zeros(BUNCH_COLUMNS)
-        x1 = transpose_and_quantise([x1_raw])
+        x0 = transpose_and_quantise(x0_raw)
+        w00 = transpose_and_quantise(w00_raw)
+        x1 = transpose_and_quantise(x1_raw)
         multiply(x0, w00, first_half, 0, 0)
-        passes_on_zeros(BUNCH_COLUMNS - real_columns)
-        w01 = transpose_and_quantise([w01_raw])
-        passes_on_zeros(BUNCH_COLUMNS)
-        w10 = transpose_and_quantise([w10_raw])
+        w01 = transpose_and_quantise(w01_raw)
+        w10 = transpose_and_quantise(w10_raw)
         multiply(x1, w01, first_half, 0, 1)
-        passes_on_zeros(BUNCH_COLUMNS - real_columns)
-        w11 = transpose_and_quantise([w11a_raw, w11b_raw])
+        store(first_half, 0)
+        w11 = transpose_and_quantise(w11_raw)
         multiply(x0, w10, second_half, 1, 0)
         multiply(x1, w11, second_half, 1, 1)
+        store(second_half, 1)

import concourse.mybir as mybir
from concourse.masks import make_identity

F32 = mybir.dt.float32
BF16 = mybir.dt.bfloat16
U32 = mybir.dt.uint32
U8 = mybir.dt.uint8
FP8X4 = mybir.dt.float8_e4m3fn_x4

P = 128
G = 8
I = 512
H = 256
QUAD = 4
B_ROWS = G * H // P

FLOPS = 2 * P * G * I * H


def tile_groupedlinear_s_kernel(tc, x, W, b, out):
    nc = tc.nc
    x_rows = x.flatten_outer_dims()
    out_rows = out.flatten_outer_dims()

    with tc.tile_pool(name="const", bufs=1) as const, tc.tile_pool(
        name="raw", bufs=6
    ) as raw_pool, tc.tile_pool(name="stage", bufs=4) as stage, tc.tile_pool(
        name="keep", bufs=6
    ) as keep, tc.tile_pool(name="result", bufs=1) as result, tc.psum_pool(
        name="flipped", bufs=4
    ) as flipped, tc.psum_pool(name="sums", bufs=4) as sums, tc.manual_schedule():

        def load_chunk(rows):
            raw = raw_pool.tile([P, QUAD * I], BF16)
            nc.sync.dma_start(out=raw[:].rearrange("p (g k) -> p g k", g=QUAD), in_=rows)
            return raw

        def x_chunk(q):
            return x_rows[:, q * QUAD * I : (q + 1) * QUAD * I].rearrange("n (g k) -> n g k", g=QUAD)

        def w_chunk(j, q):
            return W[q * QUAD : (q + 1) * QUAD, j * P : (j + 1) * P, :].rearrange("g h k -> h g k")

        b_rows = const.tile([P, P], BF16)
        nc.gpsimd.memset(b_rows[:], 0.0)
        nc.sync.dma_start(out=b_rows[0:B_ROWS, :], in_=b.rearrange("g (j h) -> (g j) h", h=P))
        x0_raw = load_chunk(x_chunk(0))
        w00_raw = load_chunk(w_chunk(0, 0))
        x1_raw = load_chunk(x_chunk(1))
        w01_raw = load_chunk(w_chunk(0, 1))
        w10_raw = load_chunk(w_chunk(1, 0))
        w11_raw = load_chunk(w_chunk(1, 1))

        ident_bf = const.tile([P, P], BF16)
        make_identity(nc, ident_bf[:])
        ident = const.tile([P, P], F32)
        make_identity(nc, ident[:])

        def transpose_and_quantise(raw):
            codes = keep.tile([P, QUAD * P], U32, align_bytes=64)
            scales = keep.tile([P, QUAD * P], U8, align_bytes=64)
            words = raw[:].bitcast(F32)
            for pair in range(QUAD // 2):
                bank = flipped.tile([P, 2, 2, P], F32, tag="bank")
                for g in range(2):
                    for u in range(2):
                        first = ((2 * pair + g) * 2 + u) * P
                        nc.tensor.transpose(bank[:, g, u, :], words[:, first : first + P], ident[:])
                grouped = stage.tile([P, 2 * P * 4], BF16, align_bytes=64)
                nc.scalar.copy(
                    out=grouped[:].bitcast(F32).rearrange("p (g r u) -> p g r u", g=2, u=2),
                    in_=bank[:].rearrange("p g u r -> p g r u"),
                )
                cols = slice(pair * 2 * P, (pair + 1) * 2 * P)
                nc.vector.quantize_mx(
                    out=codes[:, cols].bitcast(FP8X4), scales=scales[:, cols], in_=grouped[:]
                )
            return codes, scales

        def spread_bias():
            b_flipped = flipped.tile([P, P], BF16, tag="bank")
            nc.tensor.transpose(b_flipped[:], b_rows[:], ident_bf[:])
            b_cols = const.tile([P, B_ROWS], BF16)
            nc.vector.tensor_copy(out=b_cols[:], in_=b_flipped[:, 0:B_ROWS])
            bias = const.tile([P, G * H], BF16)
            for half in range(2):
                spread = flipped.tile([P, B_ROWS // 2, P], BF16, tag="bank")
                for k in range(B_ROWS // 2):
                    c = half * (B_ROWS // 2) + k
                    nc.tensor.transpose(
                        spread[:, k, :], b_cols[:, c : c + 1].to_broadcast([P, P]), ident_bf[:]
                    )
                nc.vector.tensor_copy(
                    out=bias[:, half * G * P : (half + 1) * G * P],
                    in_=spread[:].rearrange("p k n -> p (k n)"),
                )
            return bias[:].rearrange("p (g h) -> p g h", g=G)

        def multiply(x_mx, w_mx, shuffled, j, q):
            x_codes, x_scales = x_mx
            w_codes, w_scales = w_mx
            acc = sums.tile([P, QUAD, P], F32)
            for g in range(QUAD):
                cols = slice(g * P, (g + 1) * P)
                nc.tensor.matmul_mx(
                    out=acc[:, g, :],
                    lhsT=x_codes[:, cols].bitcast(FP8X4),
                    lhsT_scale=x_scales[:, cols],
                    rhs=w_codes[:, cols].bitcast(FP8X4),
                    rhs_scale=w_scales[:, cols],
                    start=True,
                    stop=True,
                )
            groups = slice(q * QUAD, (q + 1) * QUAD)
            nc.vector.tensor_tensor(
                out=shuffled[:, :, groups],
                in0=acc[:].rearrange("p g h -> p h g"),
                in1=bias_gh[:, groups, j * P : (j + 1) * P].rearrange("p g h -> p h g"),
                op=mybir.AluOpType.add,
            )

        def store(shuffled, j):
            nc.sync.dma_start(
                out=out_rows[:, j * P * G : (j + 1) * P * G],
                in_=shuffled[:].rearrange("p h g -> p (h g)"),
            )

        first_half = result.tile([P, P, G], F32)
        second_half = result.tile([P, P, G], F32)
        bias_gh = spread_bias()
        x0 = transpose_and_quantise(x0_raw)
        w00 = transpose_and_quantise(w00_raw)
        x1 = transpose_and_quantise(x1_raw)
        multiply(x0, w00, first_half, 0, 0)
        w01 = transpose_and_quantise(w01_raw)
        w10 = transpose_and_quantise(w10_raw)
        multiply(x1, w01, first_half, 0, 1)
        store(first_half, 0)
        w11 = transpose_and_quantise(w11_raw)
        multiply(x0, w10, second_half, 1, 0)
        multiply(x1, w11, second_half, 1, 1)
        store(second_half, 1)
